import numpy as np
import ml_dtypes


def mxq(x, axis, fmt="e4m3"):
    dtype, down = {"e4m3": (ml_dtypes.float8_e4m3fn, 7), "e5m2": (ml_dtypes.float8_e5m2, 14)}[fmt]
    v = np.moveaxis(np.asarray(x, np.float32).astype(ml_dtypes.bfloat16).astype(np.float64), axis, -1)
    blocks = v.reshape(v.shape[:-1] + (-1, 32))
    amax = np.abs(blocks).max(-1, keepdims=True)
    byte = np.maximum(np.where(amax > 0, np.frexp(amax)[1] - 1 + 127, 0) - down, 1)
    scale = np.exp2(byte - 127.0)
    codes = (blocks / scale).astype(np.float32).astype(dtype).astype(np.float64)
    return np.moveaxis((codes * scale).reshape(v.shape), -1, axis)


WIDE = False


def mx_kscale(k):
    if not WIDE:
        return np.ones(k)
    levels = np.array([20, -20, 10, -10, 0])
    a = np.random.permutation(np.resize(levels, k // 512 * 4)).reshape(k // 512, 4)
    idx = np.arange(k)
    return np.exp2(a[idx // 512, idx % 128 // 32])


BF16 = ml_dtypes.bfloat16


def bf(x):
    return np.asarray(x, np.float32).astype(BF16)


def f64(x):
    return np.asarray(x).astype(np.float64)


B, A, E, P, R = 512, 8, 512, 512, 512


def setup_inputs():
    s = mx_kscale(B)
    a0 = bf(np.random.standard_normal((B, A, R)))
    w = bf(np.random.standard_normal((A, R, P)) / np.sqrt(R))
    sw = bf(1.0 + 0.3 * np.random.standard_normal((1, A, 1)))
    g = bf(np.random.standard_normal((B, P)) * np.exp2(np.random.randint(-12, 1, (B, 1))) / s[:, None])
    proj = (f64(a0).transpose(1, 0, 2) @ f64(w)).transpose(1, 0, 2)
    return {
        "attr_rep": bf(f64(a0) * s[:, None, None]),
        "bwd_proj": w,
        "self_weighted": sw,
        "proj": np.asarray(proj, np.float32),
        "grad_out": g,
    }


def reference(attr_rep, bwd_proj, self_weighted, proj, grad_out):
    mask = np.where(f64(proj) > 0.0, 1.0, 0.0)
    dproj = f64(grad_out)[:, None, :] * f64(self_weighted) * mask
    xa = f64(attr_rep).transpose(1, 2, 0)
    da = dproj.transpose(1, 0, 2)
    return mxq(xa, 2, "e4m3") @ mxq(da, 1, "e5m2")

@@ -1,0 +1,165 @@
+from contextlib import ExitStack
+
+import concourse.mybir as mybir
+
+BF16 = mybir.dt.bfloat16
+F32 = mybir.dt.float32
+U32 = mybir.dt.uint32
+U8 = mybir.dt.uint8
+E4M3_X4 = mybir.dt.float8_e4m3fn_x4
+E5M2_X4 = mybir.dt.float8_e5m2_x4
+ALU = mybir.AluOpType
+
+NODES = 512
+TYPES = 8
+REP = 512
+PROJ = 512
+
+PART = 128
+PACK = 4
+RUN = 4
+ROW_TILES = REP // PART
+TYPES_PER_LOAD = 2
+LOADS = TYPES // TYPES_PER_LOAD
+
+FLOPS = 2 * TYPES * REP * PROJ * NODES
+BYTES = 2 * NODES * TYPES * REP + 2 * TYPES + 4 * NODES * TYPES * PROJ + 2 * NODES * PROJ + 4 * TYPES * REP * PROJ
+
+assert NODES == PART * PACK
+
+
+def same_walk(rows, words):
+    return (
+        rows.rearrange("p t (w i) -> p w t i", i=RUN),
+        words.rearrange("p (w i) t -> p w t i", i=RUN),
+    )
+
+
+def tile_attributegnn_pb_v_kernel(
+    tc, attr_rep, bwd_proj, self_weighted, proj, grad_out, out
+):
+    nc = tc.nc
+    attr_by_partition = attr_rep.rearrange("(p t) a r -> p t a r", t=PACK)
+    proj_by_partition = proj.rearrange("(p t) a c -> p t a c", t=PACK)
+
+    with ExitStack() as ctx:
+        consts = ctx.enter_context(tc.tile_pool(name="consts", bufs=1))
+        loads = ctx.enter_context(tc.tile_pool(name="loads", bufs=LOADS))
+        grouped = ctx.enter_context(tc.tile_pool(name="grouped", bufs=2))
+        quantised = ctx.enter_context(tc.tile_pool(name="quantised", bufs=3))
+        results = ctx.enter_context(tc.tile_pool(name="results", bufs=TYPES))
+        psum = ctx.enter_context(tc.psum_pool(name="psum", bufs=8))
+
+        weight_bf16 = consts.tile([PART, TYPES], BF16)
+        nc.scalar.dma_start(
+            out=weight_bf16[:],
+            in_=self_weighted.rearrange("o a u -> (o a u)").partition_broadcast(PART),
+        )
+        grad_rows = consts.tile([PART, PACK, PROJ], BF16)
+        nc.sync.dma_start(out=grad_rows[:], in_=grad_out.rearrange("(p t) c -> p t c", t=PACK))
+        attr_loads = []
+        proj_loads = []
+        for load in range(LOADS):
+            types = slice(load * TYPES_PER_LOAD, (load + 1) * TYPES_PER_LOAD)
+            attr_rows = loads.tile([PART, PACK, TYPES_PER_LOAD, REP], BF16)
+            nc.sync.dma_start(out=attr_rows[:], in_=attr_by_partition[:, :, types, :])
+            attr_loads.append(attr_rows)
+            proj_rows = loads.tile([PART, PACK, TYPES_PER_LOAD, PROJ], F32)
+            nc.sync.dma_start(out=proj_rows[:], in_=proj_by_partition[:, :, types, :])
+            proj_loads.append(proj_rows)
+
+        weight = consts.tile([PART, TYPES], F32)
+        nc.vector.tensor_copy(out=weight[:], in_=weight_bf16[:])
+        grad_grouped = consts.tile([PART, PROJ, PACK], BF16)
+        grad_src, grad_dst = same_walk(grad_rows[:], grad_grouped[:])
+        nc.vector.tensor_copy(out=grad_dst, in_=grad_src)
+
+        attr_grouped_of = {}
+        gate_of = {}
+        dproj_of = {}
+        attr_mx_of = {}
+        dproj_mx_of = {}
+
+        def regroup_attr(a):
+            attr_grouped = grouped.tile([PART, REP, PACK], BF16, align_bytes=64)
+            src, dst = same_walk(
+                attr_loads[a // TYPES_PER_LOAD][:, :, a % TYPES_PER_LOAD, :], attr_grouped[:]
+            )
+            nc.scalar.copy(out=dst, in_=src)
+            attr_grouped_of[a] = attr_grouped
+
+        def weighted_gate(a):
+            gate = grouped.tile([PART, PROJ, PACK], BF16)
+            src, dst = same_walk(
+                proj_loads[a // TYPES_PER_LOAD][:, :, a % TYPES_PER_LOAD, :], gate[:]
+            )
+            nc.vector.tensor_scalar(
+                out=dst,
+                in0=src,
+                scalar1=0.0,
+                scalar2=weight[:, a : a + 1],
+                op0=ALU.is_gt,
+                op1=ALU.mult,
+            )
+            gate_of[a] = gate
+
+        def quantise_attr(a):
+            attr_codes = quantised.tile([PART, REP], U32, align_bytes=64)
+            attr_scales = quantised.tile([PART, REP], U8, align_bytes=64)
+            nc.vector.quantize_mx(
+                out=attr_codes[:].bitcast(E4M3_X4),
+                scales=attr_scales[:],
+                in_=attr_grouped_of[a][:].rearrange("p w t -> p (w t)"),
+            )
+            attr_mx_of[a] = (attr_codes, attr_scales)
+
+        def gradient(a):
+            dproj = grouped.tile([PART, PROJ * PACK], BF16, align_bytes=64)
+            nc.vector.tensor_tensor(
+                out=dproj[:],
+                in0=gate_of[a][:].rearrange("p w t -> p (w t)"),
+                in1=grad_grouped[:].rearrange("p w t -> p (w t)"),
+                op=ALU.mult,
+            )
+            dproj_of[a] = dproj
+
+        def quantise_dproj(a):
+            dproj_codes = quantised.tile([PART, PROJ], U32, align_bytes=64)
+            dproj_scales = quantised.tile([PART, PROJ], U8, align_bytes=64)
+            nc.vector.quantize_mx(
+                out=dproj_codes[:].bitcast(E5M2_X4),
+                scales=dproj_scales[:],
+                in_=dproj_of[a][:],
+            )
+            dproj_mx_of[a] = (dproj_codes, dproj_scales)
+
+        def multiply_and_store(a):
+            attr_codes, attr_scales = attr_mx_of[a]
+            dproj_codes, dproj_scales = dproj_mx_of[a]
+            result = results.tile([PART, ROW_TILES, PROJ], F32)
+            for m in range(ROW_TILES):
+                rows = slice(m * PART, (m + 1) * PART)
+                acc = psum.tile([PART, PROJ], F32)
+                nc.tensor.matmul_mx(
+                    out=acc[:],
+                    lhsT=attr_codes[:, rows].bitcast(E4M3_X4),
+                    lhsT_scale=attr_scales[:, rows],
+                    rhs=dproj_codes[:].bitcast(E5M2_X4),
+                    rhs_scale=dproj_scales[:],
+                    start=True,
+                    stop=True,
+                )
+                nc.scalar.copy(out=result[:, m, :], in_=acc[:])
+            nc.sync.dma_start(out=out[a].rearrange("(m p) c -> p m c", p=PART), in_=result[:])
+
+        regroup_attr(0)
+        weighted_gate(0)
+        for a in range(TYPES):
+            if a + 1 < TYPES:
+                regroup_attr(a + 1)
+            quantise_attr(a)
+            gradient(a)
+            if a + 1 < TYPES:
+                weighted_gate(a + 1)
+            quantise_dproj(a)
+            multiply_and_store(a)

@@ -81,11 +81,12 @@ def tile_attributegnn_pb_v_kernel(
         dproj_mx_of = {}
 
         def regroup_attr(a):
-            attr_grouped = grouped.tile([PART, REP, PACK], BF16, align_bytes=64)
-            src, dst = same_walk(
-                attr_loads[a // TYPES_PER_LOAD][:, :, a % TYPES_PER_LOAD, :], attr_grouped[:]
+            attr_grouped = grouped.tile([PART, ROW_TILES, PART, PACK], BF16, align_bytes=64)
+            attr_rows = attr_loads[a // TYPES_PER_LOAD][:, :, a % TYPES_PER_LOAD, :]
+            nc.scalar.copy(
+                out=attr_grouped[:].rearrange("p m w t -> p w t m"),
+                in_=attr_rows.rearrange("p t (w m) -> p w t m", m=ROW_TILES),
             )
-            nc.scalar.copy(out=dst, in_=src)
             attr_grouped_of[a] = attr_grouped
 
         def weighted_gate(a):
@@ -109,7 +110,7 @@ def tile_attributegnn_pb_v_kernel(
             nc.vector.quantize_mx(
                 out=attr_codes[:].bitcast(E4M3_X4),
                 scales=attr_scales[:],
-                in_=attr_grouped_of[a][:].rearrange("p w t -> p (w t)"),
+                in_=attr_grouped_of[a][:].rearrange("p m w t -> p (m w t)"),
             )
             attr_mx_of[a] = (attr_codes, attr_scales)
 
@@ -150,7 +151,7 @@ def tile_attributegnn_pb_v_kernel(
                     stop=True,
                 )
                 nc.scalar.copy(out=result[:, m, :], in_=acc[:])
-            nc.sync.dma_start(out=out[a].rearrange("(m p) c -> p m c", p=PART), in_=result[:])
+            nc.sync.dma_start(out=out[a].rearrange("(p m) c -> p m c", m=ROW_TILES), in_=result[:])
 
         regroup_attr(0)
         weighted_gate(0)

@@ -21,18 +21,13 @@ RUN = 4
 ROW_TILES = REP // PART
 TYPES_PER_LOAD = 2
 LOADS = TYPES // TYPES_PER_LOAD
+VECTOR_ROW_TILES = 1
 
 FLOPS = 2 * TYPES * REP * PROJ * NODES
 BYTES = 2 * NODES * TYPES * REP + 2 * TYPES + 4 * NODES * TYPES * PROJ + 2 * NODES * PROJ + 4 * TYPES * REP * PROJ
 
 assert NODES == PART * PACK
-
-
-def same_walk(rows, words):
-    return (
-        rows.rearrange("p t (w i) -> p w t i", i=RUN),
-        words.rearrange("p (w i) t -> p w t i", i=RUN),
-    )
+assert TYPES_PER_LOAD == 2
 
 
 def tile_attributegnn_pb_v_kernel(
@@ -45,10 +40,11 @@ def tile_attributegnn_pb_v_kernel(
     with ExitStack() as ctx:
         consts = ctx.enter_context(tc.tile_pool(name="consts", bufs=1))
         loads = ctx.enter_context(tc.tile_pool(name="loads", bufs=LOADS))
-        grouped = ctx.enter_context(tc.tile_pool(name="grouped", bufs=2))
-        quantised = ctx.enter_context(tc.tile_pool(name="quantised", bufs=3))
+        on_vector = ctx.enter_context(tc.tile_pool(name="on_vector", bufs=TYPES_PER_LOAD))
+        shared = ctx.enter_context(tc.tile_pool(name="shared", bufs=2 * TYPES_PER_LOAD))
         results = ctx.enter_context(tc.tile_pool(name="results", bufs=TYPES))
         psum = ctx.enter_context(tc.psum_pool(name="psum", bufs=8))
+        ctx.enter_context(tc.manual_schedule())
 
         weight_bf16 = consts.tile([PART, TYPES], BF16)
         nc.scalar.dma_start(
@@ -56,23 +52,23 @@ def tile_attributegnn_pb_v_kernel(
             in_=self_weighted.rearrange("o a u -> (o a u)").partition_broadcast(PART),
         )
         grad_rows = consts.tile([PART, PACK, PROJ], BF16)
-        nc.sync.dma_start(out=grad_rows[:], in_=grad_out.rearrange("(p t) c -> p t c", t=PACK))
         attr_loads = []
         proj_loads = []
         for load in range(LOADS):
             types = slice(load * TYPES_PER_LOAD, (load + 1) * TYPES_PER_LOAD)
-            attr_rows = loads.tile([PART, PACK, TYPES_PER_LOAD, REP], BF16)
-            nc.sync.dma_start(out=attr_rows[:], in_=attr_by_partition[:, :, types, :])
-            attr_loads.append(attr_rows)
             proj_rows = loads.tile([PART, PACK, TYPES_PER_LOAD, PROJ], F32)
             nc.sync.dma_start(out=proj_rows[:], in_=proj_by_partition[:, :, types, :])
             proj_loads.append(proj_rows)
+            if load == 0:
+                nc.sync.dma_start(
+                    out=grad_rows[:], in_=grad_out.rearrange("(p t) c -> p t c", t=PACK)
+                )
+            attr_rows = loads.tile([PART, PACK, TYPES_PER_LOAD, REP], BF16)
+            nc.sync.dma_start(out=attr_rows[:], in_=attr_by_partition[:, :, types, :])
+            attr_loads.append(attr_rows)
 
         weight = consts.tile([PART, TYPES], F32)
         nc.vector.tensor_copy(out=weight[:], in_=weight_bf16[:])
-        grad_grouped = consts.tile([PART, PROJ, PACK], BF16)
-        grad_src, grad_dst = same_walk(grad_rows[:], grad_grouped[:])
-        nc.vector.tensor_copy(out=grad_dst, in_=grad_src)
 
         attr_grouped_of = {}
         gate_of = {}
@@ -80,23 +76,12 @@ def tile_attributegnn_pb_v_kernel(
         attr_mx_of = {}
         dproj_mx_of = {}
 
-        def regroup_attr(a):
-            attr_grouped = grouped.tile([PART, ROW_TILES, PART, PACK], BF16, align_bytes=64)
-            attr_rows = attr_loads[a // TYPES_PER_LOAD][:, :, a % TYPES_PER_LOAD, :]
-            nc.scalar.copy(
-                out=attr_grouped[:].rearrange("p m w t -> p w t m"),
-                in_=attr_rows.rearrange("p t (w m) -> p w t m", m=ROW_TILES),
-            )
-            attr_grouped_of[a] = attr_grouped
-
         def weighted_gate(a):
-            gate = grouped.tile([PART, PROJ, PACK], BF16)
-            src, dst = same_walk(
-                proj_loads[a // TYPES_PER_LOAD][:, :, a % TYPES_PER_LOAD, :], gate[:]
-            )
+            gate = on_vector.tile([PART, PROJ, PACK], BF16)
+            proj_rows = proj_loads[a // TYPES_PER_LOAD][:, :, a % TYPES_PER_LOAD, :]
             nc.vector.tensor_scalar(
-                out=dst,
-                in0=src,
+                out=gate[:].rearrange("p (w i) t -> p w t i", i=RUN),
+                in0=proj_rows.rearrange("p t (w i) -> p w t i", i=RUN),
                 scalar1=0.0,
                 scalar2=weight[:, a : a + 1],
                 op0=ALU.is_gt,
@@ -104,18 +89,8 @@ def tile_attributegnn_pb_v_kernel(
             )
             gate_of[a] = gate
 
-        def quantise_attr(a):
-            attr_codes = quantised.tile([PART, REP], U32, align_bytes=64)
-            attr_scales = quantised.tile([PART, REP], U8, align_bytes=64)
-            nc.vector.quantize_mx(
-                out=attr_codes[:].bitcast(E4M3_X4),
-                scales=attr_scales[:],
-                in_=attr_grouped_of[a][:].rearrange("p m w t -> p (m w t)"),
-            )
-            attr_mx_of[a] = (attr_codes, attr_scales)
-
         def gradient(a):
-            dproj = grouped.tile([PART, PROJ * PACK], BF16, align_bytes=64)
+            dproj = on_vector.tile([PART, PROJ * PACK], BF16, align_bytes=64)
             nc.vector.tensor_tensor(
                 out=dproj[:],
                 in0=gate_of[a][:].rearrange("p w t -> p (w t)"),
@@ -124,9 +99,22 @@ def tile_attributegnn_pb_v_kernel(
             )
             dproj_of[a] = dproj
 
+        def regroup_attr(a):
+            attr_grouped = shared.tile([PART, ROW_TILES, PART, PACK], BF16, align_bytes=64)
+            attr_rows = attr_loads[a // TYPES_PER_LOAD][:, :, a % TYPES_PER_LOAD, :]
+            by_row_tile = attr_rows.rearrange("p t (w m) -> p m w t", m=ROW_TILES)
+            nc.vector.tensor_copy(
+                out=attr_grouped[:, :VECTOR_ROW_TILES], in_=by_row_tile[:, :VECTOR_ROW_TILES]
+            )
+            nc.scalar.copy(
+                out=attr_grouped[:, VECTOR_ROW_TILES:].rearrange("p m w t -> p w t m"),
+                in_=by_row_tile[:, VECTOR_ROW_TILES:].rearrange("p m w t -> p w t m"),
+            )
+            attr_grouped_of[a] = attr_grouped
+
         def quantise_dproj(a):
-            dproj_codes = quantised.tile([PART, PROJ], U32, align_bytes=64)
-            dproj_scales = quantised.tile([PART, PROJ], U8, align_bytes=64)
+            dproj_codes = shared.tile([PART, PROJ], U32, align_bytes=64)
+            dproj_scales = shared.tile([PART, PROJ], U8, align_bytes=64)
             nc.vector.quantize_mx(
                 out=dproj_codes[:].bitcast(E5M2_X4),
                 scales=dproj_scales[:],
@@ -134,17 +122,27 @@ def tile_attributegnn_pb_v_kernel(
             )
             dproj_mx_of[a] = (dproj_codes, dproj_scales)
 
+        def quantise_attr(a):
+            attr_codes = shared.tile([PART, REP], U32, align_bytes=64)
+            attr_scales = shared.tile([PART, REP], U8, align_bytes=64)
+            nc.vector.quantize_mx(
+                out=attr_codes[:].bitcast(E4M3_X4),
+                scales=attr_scales[:],
+                in_=attr_grouped_of[a][:].rearrange("p m w t -> p (m w t)"),
+            )
+            attr_mx_of[a] = (attr_codes, attr_scales)
+
         def multiply_and_store(a):
             attr_codes, attr_scales = attr_mx_of[a]
             dproj_codes, dproj_scales = dproj_mx_of[a]
             result = results.tile([PART, ROW_TILES, PROJ], F32)
             for m in range(ROW_TILES):
-                rows = slice(m * PART, (m + 1) * PART)
+                places = slice(m * PART, (m + 1) * PART)
                 acc = psum.tile([PART, PROJ], F32)
                 nc.tensor.matmul_mx(
                     out=acc[:],
-                    lhsT=attr_codes[:, rows].bitcast(E4M3_X4),
-                    lhsT_scale=attr_scales[:, rows],
+                    lhsT=attr_codes[:, places].bitcast(E4M3_X4),
+                    lhsT_scale=attr_scales[:, places],
                     rhs=dproj_codes[:].bitcast(E5M2_X4),
                     rhs_scale=dproj_scales[:],
                     start=True,
@@ -153,14 +151,24 @@ def tile_attributegnn_pb_v_kernel(
                 nc.scalar.copy(out=result[:, m, :], in_=acc[:])
             nc.sync.dma_start(out=out[a].rearrange("(p m) c -> p m c", m=ROW_TILES), in_=result[:])
 
-        regroup_attr(0)
-        weighted_gate(0)
-        for a in range(TYPES):
-            if a + 1 < TYPES:
-                regroup_attr(a + 1)
-            quantise_attr(a)
-            gradient(a)
-            if a + 1 < TYPES:
-                weighted_gate(a + 1)
-            quantise_dproj(a)
-            multiply_and_store(a)
+        for load in range(LOADS):
+            first = load * TYPES_PER_LOAD
+            second = first + 1
+            weighted_gate(first)
+            weighted_gate(second)
+            if load == 0:
+                grad_grouped = consts.tile([PART, PROJ, PACK], BF16)
+                nc.vector.tensor_copy(
+                    out=grad_grouped[:].rearrange("p (w i) t -> p w t i", i=RUN),
+                    in_=grad_rows[:].rearrange("p t (w i) -> p w t i", i=RUN),
+                )
+            gradient(first)
+            regroup_attr(first)
+            regroup_attr(second)
+            quantise_dproj(first)
+            quantise_attr(first)
+            multiply_and_store(first)
+            gradient(second)
+            quantise_attr(second)
+            quantise_dproj(second)
+            multiply_and_store(second)

@@ -136,6 +136,8 @@ def tile_attributegnn_pb_v_kernel(
             attr_codes, attr_scales = attr_mx_of[a]
             dproj_codes, dproj_scales = dproj_mx_of[a]
             result = results.tile([PART, ROW_TILES, PROJ], F32)
+            out_rows = out[a].rearrange("(p m) c -> p m c", m=ROW_TILES)
+            last = a == TYPES - 1
             for m in range(ROW_TILES):
                 places = slice(m * PART, (m + 1) * PART)
                 acc = psum.tile([PART, PROJ], F32)
@@ -148,8 +150,13 @@ def tile_attributegnn_pb_v_kernel(
                     start=True,
                     stop=True,
                 )
-                nc.scalar.copy(out=result[:, m, :], in_=acc[:])
-            nc.sync.dma_start(out=out[a].rearrange("(p m) c -> p m c", m=ROW_TILES), in_=result[:])
+                if last and m % 2 == 1:
+                    nc.vector.tensor_copy(out=result[:, m, :], in_=acc[:])
+                    nc.sync.dma_start(out=out_rows[:, m - 1 : m + 1, :], in_=result[:, m - 1 : m + 1, :])
+                else:
+                    nc.scalar.copy(out=result[:, m, :], in_=acc[:])
+            if not last:
+                nc.sync.dma_start(out=out_rows, in_=result[:])
 
         for load in range(LOADS):
             first = load * TYPES_PER_LOAD

@@ -21,6 +21,8 @@ RUN = 4
 ROW_TILES = REP // PART
 TYPES_PER_LOAD = 2
 LOADS = TYPES // TYPES_PER_LOAD
+TYPES_PER_ATTR_LOAD = 4
+ATTR_LOADS = TYPES // TYPES_PER_ATTR_LOAD
 VECTOR_ROW_TILES = 1
 
 FLOPS = 2 * TYPES * REP * PROJ * NODES
@@ -40,6 +42,7 @@ def tile_attributegnn_pb_v_kernel(
     with ExitStack() as ctx:
         consts = ctx.enter_context(tc.tile_pool(name="consts", bufs=1))
         loads = ctx.enter_context(tc.tile_pool(name="loads", bufs=LOADS))
+        attr_pool = ctx.enter_context(tc.tile_pool(name="attr_pool", bufs=ATTR_LOADS))
         on_vector = ctx.enter_context(tc.tile_pool(name="on_vector", bufs=TYPES_PER_LOAD))
         shared = ctx.enter_context(tc.tile_pool(name="shared", bufs=2 * TYPES_PER_LOAD))
         results = ctx.enter_context(tc.tile_pool(name="results", bufs=TYPES))
@@ -54,18 +57,26 @@ def tile_attributegnn_pb_v_kernel(
         grad_rows = consts.tile([PART, PACK, PROJ], BF16)
         attr_loads = []
         proj_loads = []
-        for load in range(LOADS):
+
+        def load_attr(load):
+            types = slice(load * TYPES_PER_ATTR_LOAD, (load + 1) * TYPES_PER_ATTR_LOAD)
+            attr_rows = attr_pool.tile([PART, PACK, TYPES_PER_ATTR_LOAD, REP], BF16)
+            nc.sync.dma_start(out=attr_rows[:], in_=attr_by_partition[:, :, types, :])
+            attr_loads.append(attr_rows)
+
+        def load_proj(load):
             types = slice(load * TYPES_PER_LOAD, (load + 1) * TYPES_PER_LOAD)
             proj_rows = loads.tile([PART, PACK, TYPES_PER_LOAD, PROJ], F32)
             nc.sync.dma_start(out=proj_rows[:], in_=proj_by_partition[:, :, types, :])
             proj_loads.append(proj_rows)
-            if load == 0:
-                nc.sync.dma_start(
-                    out=grad_rows[:], in_=grad_out.rearrange("(p t) c -> p t c", t=PACK)
-                )
-            attr_rows = loads.tile([PART, PACK, TYPES_PER_LOAD, REP], BF16)
-            nc.sync.dma_start(out=attr_rows[:], in_=attr_by_partition[:, :, types, :])
-            attr_loads.append(attr_rows)
+
+        load_attr(0)
+        nc.sync.dma_start(out=grad_rows[:], in_=grad_out.rearrange("(p t) c -> p t c", t=PACK))
+        load_proj(0)
+        load_proj(1)
+        load_attr(1)
+        load_proj(2)
+        load_proj(3)
 
         weight = consts.tile([PART, TYPES], F32)
         nc.vector.tensor_copy(out=weight[:], in_=weight_bf16[:])
@@ -101,7 +112,7 @@ def tile_attributegnn_pb_v_kernel(
 
         def regroup_attr(a):
             attr_grouped = shared.tile([PART, ROW_TILES, PART, PACK], BF16, align_bytes=64)
-            attr_rows = attr_loads[a // TYPES_PER_LOAD][:, :, a % TYPES_PER_LOAD, :]
+            attr_rows = attr_loads[a // TYPES_PER_ATTR_LOAD][:, :, a % TYPES_PER_ATTR_LOAD, :]
             by_row_tile = attr_rows.rearrange("p t (w m) -> p m w t", m=ROW_TILES)
             nc.vector.tensor_copy(
                 out=attr_grouped[:, :VECTOR_ROW_TILES], in_=by_row_tile[:, :VECTOR_ROW_TILES]
@@ -158,24 +169,34 @@ def tile_attributegnn_pb_v_kernel(
             if not last:
                 nc.sync.dma_start(out=out_rows, in_=result[:])
 
+        for a in range(TYPES_PER_ATTR_LOAD):
+            regroup_attr(a)
+        grad_grouped = consts.tile([PART, PROJ, PACK], BF16)
+        nc.vector.tensor_copy(
+            out=grad_grouped[:].rearrange("p (w i) t -> p w t i", i=RUN),
+            in_=grad_rows[:].rearrange("p t (w i) -> p w t i", i=RUN),
+        )
+        quantise_attr(0)
+        quantise_attr(1)
+
+        between = {
+            0: [(quantise_attr, 2)],
+            1: [(quantise_attr, 3)],
+            2: [(regroup_attr, 4), (regroup_attr, 5)],
+            3: [(regroup_attr, 6), (regroup_attr, 7)],
+            4: [(quantise_attr, 4)],
+            5: [(quantise_attr, 5)],
+            6: [(quantise_attr, 6)],
+            7: [(quantise_attr, 7)],
+        }
         for load in range(LOADS):
             first = load * TYPES_PER_LOAD
             second = first + 1
             weighted_gate(first)
             weighted_gate(second)
-            if load == 0:
-                grad_grouped = consts.tile([PART, PROJ, PACK], BF16)
-                nc.vector.tensor_copy(
-                    out=grad_grouped[:].rearrange("p (w i) t -> p w t i", i=RUN),
-                    in_=grad_rows[:].rearrange("p t (w i) -> p w t i", i=RUN),
-                )
-            gradient(first)
-            regroup_attr(first)
-            regroup_attr(second)
-            quantise_dproj(first)
-            quantise_attr(first)
-            multiply_and_store(first)
-            gradient(second)
-            quantise_attr(second)
-            quantise_dproj(second)
-            multiply_and_store(second)
+            for a in (first, second):
+                gradient(a)
+                for step, other in between[a]:
+                    step(other)
+                quantise_dproj(a)
+                multiply_and_store(a)

@@ -1,6 +1,7 @@
 from contextlib import ExitStack
 
 import concourse.mybir as mybir
+from concourse.masks import make_identity
 
 BF16 = mybir.dt.bfloat16
 F32 = mybir.dt.float32
@@ -49,10 +50,12 @@ def tile_attributegnn_pb_v_kernel(
         psum = ctx.enter_context(tc.psum_pool(name="psum", bufs=8))
         ctx.enter_context(tc.manual_schedule())
 
-        weight_bf16 = consts.tile([PART, TYPES], BF16)
+        identity = consts.tile([PART, PART], BF16)
+        make_identity(nc, identity[:])
+        weight_column = consts.tile([PART, 1], BF16)
+        nc.gpsimd.memset(weight_column[:], 0.0)
         nc.scalar.dma_start(
-            out=weight_bf16[:],
-            in_=self_weighted.rearrange("o a u -> (o a u)").partition_broadcast(PART),
+            out=weight_column[0:TYPES, :], in_=self_weighted.rearrange("o a u -> (o a) u")
         )
         grad_rows = consts.tile([PART, PACK, PROJ], BF16)
         attr_loads = []
@@ -78,8 +81,16 @@ def tile_attributegnn_pb_v_kernel(
         load_proj(2)
         load_proj(3)
 
+        acc = psum.tile([PART, PROJ], F32)
+        nc.tensor.matmul(
+            out=acc[:, :TYPES],
+            lhsT=weight_column[:, 0:1].to_broadcast([PART, PART]),
+            rhs=identity[:, :TYPES],
+            start=True,
+            stop=True,
+        )
         weight = consts.tile([PART, TYPES], F32)
-        nc.vector.tensor_copy(out=weight[:], in_=weight_bf16[:])
+        nc.vector.tensor_copy(out=weight[:], in_=acc[:, :TYPES])
 
         attr_grouped_of = {}
         gate_of = {}

@@ -51,12 +51,12 @@ def tile_attributegnn_pb_v_kernel(
         ctx.enter_context(tc.manual_schedule())
 
         identity = consts.tile([PART, PART], BF16)
-        make_identity(nc, identity[:])
         weight_column = consts.tile([PART, 1], BF16)
         nc.gpsimd.memset(weight_column[:], 0.0)
         nc.scalar.dma_start(
             out=weight_column[0:TYPES, :], in_=self_weighted.rearrange("o a u -> (o a) u")
         )
+        make_identity(nc, identity[:])
         grad_rows = consts.tile([PART, PACK, PROJ], BF16)
         attr_loads = []
         proj_loads = []
@@ -81,16 +81,7 @@ def tile_attributegnn_pb_v_kernel(
         load_proj(2)
         load_proj(3)
 
-        acc = psum.tile([PART, PROJ], F32)
-        nc.tensor.matmul(
-            out=acc[:, :TYPES],
-            lhsT=weight_column[:, 0:1].to_broadcast([PART, PART]),
-            rhs=identity[:, :TYPES],
-            start=True,
-            stop=True,
-        )
         weight = consts.tile([PART, TYPES], F32)
-        nc.vector.tensor_copy(out=weight[:], in_=acc[:, :TYPES])
 
         attr_grouped_of = {}
         gate_of = {}
@@ -189,6 +180,15 @@ def tile_attributegnn_pb_v_kernel(
         )
         quantise_attr(0)
         quantise_attr(1)
+        acc = psum.tile([PART, PROJ], F32)
+        nc.tensor.matmul(
+            out=acc[:, :TYPES],
+            lhsT=weight_column[:, 0:1].to_broadcast([PART, PART]),
+            rhs=identity[:, :TYPES],
+            start=True,
+            stop=True,
+        )
+        nc.vector.tensor_copy(out=weight[:], in_=acc[:, :TYPES])
 
         between = {
             0: [(quantise_attr, 2)],

@@ -25,6 +25,7 @@ LOADS = TYPES // TYPES_PER_LOAD
 TYPES_PER_ATTR_LOAD = 4
 ATTR_LOADS = TYPES // TYPES_PER_ATTR_LOAD
 VECTOR_ROW_TILES = 1
+DMA_ALIGN = 256
 
 FLOPS = 2 * TYPES * REP * PROJ * NODES
 BYTES = 2 * NODES * TYPES * REP + 2 * TYPES + 4 * NODES * TYPES * PROJ + 2 * NODES * PROJ + 4 * TYPES * REP * PROJ
@@ -57,19 +58,21 @@ def tile_attributegnn_pb_v_kernel(
             out=weight_column[0:TYPES, :], in_=self_weighted.rearrange("o a u -> (o a) u")
         )
         make_identity(nc, identity[:])
-        grad_rows = consts.tile([PART, PACK, PROJ], BF16)
+        grad_rows = consts.tile([PART, PACK, PROJ], BF16, align_bytes=DMA_ALIGN)
         attr_loads = []
         proj_loads = []
 
         def load_attr(load):
             types = slice(load * TYPES_PER_ATTR_LOAD, (load + 1) * TYPES_PER_ATTR_LOAD)
-            attr_rows = attr_pool.tile([PART, PACK, TYPES_PER_ATTR_LOAD, REP], BF16)
+            attr_rows = attr_pool.tile(
+                [PART, PACK, TYPES_PER_ATTR_LOAD, REP], BF16, align_bytes=DMA_ALIGN
+            )
             nc.sync.dma_start(out=attr_rows[:], in_=attr_by_partition[:, :, types, :])
             attr_loads.append(attr_rows)
 
         def load_proj(load):
             types = slice(load * TYPES_PER_LOAD, (load + 1) * TYPES_PER_LOAD)
-            proj_rows = loads.tile([PART, PACK, TYPES_PER_LOAD, PROJ], F32)
+            proj_rows = loads.tile([PART, PACK, TYPES_PER_LOAD, PROJ], F32, align_bytes=DMA_ALIGN)
             nc.sync.dma_start(out=proj_rows[:], in_=proj_by_partition[:, :, types, :])
             proj_loads.append(proj_rows)
 
@@ -148,7 +151,7 @@ def tile_attributegnn_pb_v_kernel(
         def multiply_and_store(a):
             attr_codes, attr_scales = attr_mx_of[a]
             dproj_codes, dproj_scales = dproj_mx_of[a]
-            result = results.tile([PART, ROW_TILES, PROJ], F32)
+            result = results.tile([PART, ROW_TILES, PROJ], F32, align_bytes=DMA_ALIGN)
             out_rows = out[a].rearrange("(p m) c -> p m c", m=ROW_TILES)
             last = a == TYPES - 1
             for m in range(ROW_TILES):

@@ -24,7 +24,7 @@ TYPES_PER_LOAD = 2
 LOADS = TYPES // TYPES_PER_LOAD
 TYPES_PER_ATTR_LOAD = 4
 ATTR_LOADS = TYPES // TYPES_PER_ATTR_LOAD
-VECTOR_ROW_TILES = 1
+VECTOR_PLACES = 32
 DMA_ALIGN = 256
 
 FLOPS = 2 * TYPES * REP * PROJ * NODES
@@ -120,11 +120,11 @@ def tile_attributegnn_pb_v_kernel(
             attr_rows = attr_loads[a // TYPES_PER_ATTR_LOAD][:, :, a % TYPES_PER_ATTR_LOAD, :]
             by_row_tile = attr_rows.rearrange("p t (w m) -> p m w t", m=ROW_TILES)
             nc.vector.tensor_copy(
-                out=attr_grouped[:, :VECTOR_ROW_TILES], in_=by_row_tile[:, :VECTOR_ROW_TILES]
+                out=attr_grouped[:, :, :VECTOR_PLACES], in_=by_row_tile[:, :, :VECTOR_PLACES]
             )
             nc.scalar.copy(
-                out=attr_grouped[:, VECTOR_ROW_TILES:].rearrange("p m w t -> p w t m"),
-                in_=by_row_tile[:, VECTOR_ROW_TILES:].rearrange("p m w t -> p w t m"),
+                out=attr_grouped[:, :, VECTOR_PLACES:].rearrange("p m w t -> p w t m"),
+                in_=by_row_tile[:, :, VECTOR_PLACES:].rearrange("p m w t -> p w t m"),
             )
             attr_grouped_of[a] = attr_grouped
 

@@ -24,7 +24,8 @@ TYPES_PER_LOAD = 2
 LOADS = TYPES // TYPES_PER_LOAD
 TYPES_PER_ATTR_LOAD = 4
 ATTR_LOADS = TYPES // TYPES_PER_ATTR_LOAD
-VECTOR_PLACES = 32
+VECTOR_PLACES = 48
+LINE = 2
 DMA_ALIGN = 256
 
 FLOPS = 2 * TYPES * REP * PROJ * NODES
@@ -118,14 +119,11 @@ def tile_attributegnn_pb_v_kernel(
         def regroup_attr(a):
             attr_grouped = shared.tile([PART, ROW_TILES, PART, PACK], BF16, align_bytes=64)
             attr_rows = attr_loads[a // TYPES_PER_ATTR_LOAD][:, :, a % TYPES_PER_ATTR_LOAD, :]
-            by_row_tile = attr_rows.rearrange("p t (w m) -> p m w t", m=ROW_TILES)
-            nc.vector.tensor_copy(
-                out=attr_grouped[:, :, :VECTOR_PLACES], in_=by_row_tile[:, :, :VECTOR_PLACES]
-            )
-            nc.scalar.copy(
-                out=attr_grouped[:, :, VECTOR_PLACES:].rearrange("p m w t -> p w t m"),
-                in_=by_row_tile[:, :, VECTOR_PLACES:].rearrange("p m w t -> p w t m"),
-            )
+            by_line = attr_rows.rearrange("p t (w i m) -> p w t i m", i=LINE, m=ROW_TILES)
+            grouped_by_line = attr_grouped[:].rearrange("p m (w i) t -> p w t i m", i=LINE)
+            cut = VECTOR_PLACES // LINE
+            nc.vector.tensor_copy(out=grouped_by_line[:, :cut], in_=by_line[:, :cut])
+            nc.scalar.copy(out=grouped_by_line[:, cut:], in_=by_line[:, cut:])
             attr_grouped_of[a] = attr_grouped
 
         def quantise_dproj(a):

@@ -26,6 +26,7 @@ TYPES_PER_ATTR_LOAD = 4
 ATTR_LOADS = TYPES // TYPES_PER_ATTR_LOAD
 VECTOR_PLACES = 48
 LINE = 2
+JOINED = 3
 DMA_ALIGN = 256
 
 FLOPS = 2 * TYPES * REP * PROJ * NODES
@@ -48,7 +49,7 @@ def tile_attributegnn_pb_v_kernel(
         attr_pool = ctx.enter_context(tc.tile_pool(name="attr_pool", bufs=ATTR_LOADS))
         on_vector = ctx.enter_context(tc.tile_pool(name="on_vector", bufs=TYPES_PER_LOAD))
         shared = ctx.enter_context(tc.tile_pool(name="shared", bufs=2 * TYPES_PER_LOAD))
-        results = ctx.enter_context(tc.tile_pool(name="results", bufs=TYPES))
+        results = ctx.enter_context(tc.tile_pool(name="results", bufs=1))
         psum = ctx.enter_context(tc.psum_pool(name="psum", bufs=8))
         ctx.enter_context(tc.manual_schedule())
 
@@ -92,6 +93,7 @@ def tile_attributegnn_pb_v_kernel(
         dproj_of = {}
         attr_mx_of = {}
         dproj_mx_of = {}
+        result_of = {}
 
         def weighted_gate(a):
             gate = on_vector.tile([PART, PROJ, PACK], BF16)
@@ -149,8 +151,15 @@ def tile_attributegnn_pb_v_kernel(
         def multiply_and_store(a):
             attr_codes, attr_scales = attr_mx_of[a]
             dproj_codes, dproj_scales = dproj_mx_of[a]
-            result = results.tile([PART, ROW_TILES, PROJ], F32, align_bytes=DMA_ALIGN)
-            out_rows = out[a].rearrange("(p m) c -> p m c", m=ROW_TILES)
+            if a < JOINED:
+                first, count = 0, JOINED
+            else:
+                first, count = a, 1
+            if a == first:
+                result_of[first] = results.tile(
+                    [PART, count, ROW_TILES, PROJ], F32, align_bytes=DMA_ALIGN, name="result_%d" % first
+                )
+            result = result_of[first][:, a - first]
             last = a == TYPES - 1
             for m in range(ROW_TILES):
                 places = slice(m * PART, (m + 1) * PART)
@@ -166,11 +175,13 @@ def tile_attributegnn_pb_v_kernel(
                 )
                 if last and m % 2 == 1:
                     nc.vector.tensor_copy(out=result[:, m, :], in_=acc[:])
-                    nc.sync.dma_start(out=out_rows[:, m - 1 : m + 1, :], in_=result[:, m - 1 : m + 1, :])
                 else:
                     nc.scalar.copy(out=result[:, m, :], in_=acc[:])
-            if not last:
-                nc.sync.dma_start(out=out_rows, in_=result[:])
+            if a == first + count - 1:
+                nc.sync.dma_start(
+                    out=out[first : first + count].rearrange("a (p m) c -> p a m c", m=ROW_TILES),
+                    in_=result_of[first][:],
+                )
 
         for a in range(TYPES_PER_ATTR_LOAD):
             regroup_attr(a)

@@ -24,9 +24,9 @@ TYPES_PER_LOAD = 2
 LOADS = TYPES // TYPES_PER_LOAD
 TYPES_PER_ATTR_LOAD = 4
 ATTR_LOADS = TYPES // TYPES_PER_ATTR_LOAD
-VECTOR_PLACES = 48
+VECTOR_PLACES = (64, 48)
 LINE = 2
-JOINED = 3
+STORES = ((0, 1, 2), (3, 4), (5,), (6,), (7,))
 DMA_ALIGN = 256
 
 FLOPS = 2 * TYPES * REP * PROJ * NODES
@@ -123,7 +123,7 @@ def tile_attributegnn_pb_v_kernel(
             attr_rows = attr_loads[a // TYPES_PER_ATTR_LOAD][:, :, a % TYPES_PER_ATTR_LOAD, :]
             by_line = attr_rows.rearrange("p t (w i m) -> p w t i m", i=LINE, m=ROW_TILES)
             grouped_by_line = attr_grouped[:].rearrange("p m (w i) t -> p w t i m", i=LINE)
-            cut = VECTOR_PLACES // LINE
+            cut = VECTOR_PLACES[a // TYPES_PER_ATTR_LOAD] // LINE
             nc.vector.tensor_copy(out=grouped_by_line[:, :cut], in_=by_line[:, :cut])
             nc.scalar.copy(out=grouped_by_line[:, cut:], in_=by_line[:, cut:])
             attr_grouped_of[a] = attr_grouped
@@ -151,10 +151,8 @@ def tile_attributegnn_pb_v_kernel(
         def multiply_and_store(a):
             attr_codes, attr_scales = attr_mx_of[a]
             dproj_codes, dproj_scales = dproj_mx_of[a]
-            if a < JOINED:
-                first, count = 0, JOINED
-            else:
-                first, count = a, 1
+            group = [types for types in STORES if a in types][0]
+            first, count = group[0], len(group)
             if a == first:
                 result_of[first] = results.tile(
                     [PART, count, ROW_TILES, PROJ], F32, align_bytes=DMA_ALIGN, name="result_%d" % first
@@ -186,9 +184,9 @@ def tile_attributegnn_pb_v_kernel(
         for a in range(TYPES_PER_ATTR_LOAD):
             regroup_attr(a)
         grad_grouped = consts.tile([PART, PROJ, PACK], BF16)
-        nc.vector.tensor_copy(
-            out=grad_grouped[:].rearrange("p (w i) t -> p w t i", i=RUN),
-            in_=grad_rows[:].rearrange("p t (w i) -> p w t i", i=RUN),
+        nc.scalar.copy(
+            out=grad_grouped[:].rearrange("p (w i) t -> p w t i", i=LINE * PACK),
+            in_=grad_rows[:].rearrange("p t (w i) -> p w t i", i=LINE * PACK),
         )
         quantise_attr(0)
         quantise_attr(1)
@@ -201,25 +199,32 @@ def tile_attributegnn_pb_v_kernel(
             stop=True,
         )
         nc.vector.tensor_copy(out=weight[:], in_=acc[:, :TYPES])
+        quantise_attr(2)
+        quantise_attr(3)
+        weighted_gate(0)
 
-        between = {
-            0: [(quantise_attr, 2)],
-            1: [(quantise_attr, 3)],
-            2: [(regroup_attr, 4), (regroup_attr, 5)],
-            3: [(regroup_attr, 6), (regroup_attr, 7)],
-            4: [(quantise_attr, 4)],
-            5: [(quantise_attr, 5)],
+        before = {
+            0: [(weighted_gate, 1)],
+            2: [(weighted_gate, 3)],
+            3: [(regroup_attr, 5)],
+            4: [(weighted_gate, 4), (quantise_attr, 4)],
+            5: [(regroup_attr, 7), (quantise_attr, 5)],
             6: [(quantise_attr, 6)],
+        }
+        between = {
+            1: [(weighted_gate, 2)],
+            2: [(regroup_attr, 4)],
+            3: [(regroup_attr, 6)],
+            4: [(weighted_gate, 5)],
+            5: [(weighted_gate, 6)],
+            6: [(weighted_gate, 7)],
             7: [(quantise_attr, 7)],
         }
-        for load in range(LOADS):
-            first = load * TYPES_PER_LOAD
-            second = first + 1
-            weighted_gate(first)
-            weighted_gate(second)
-            for a in (first, second):
-                gradient(a)
-                for step, other in between[a]:
-                    step(other)
-                quantise_dproj(a)
-                multiply_and_store(a)
+        for a in range(TYPES):
+            for step, other in before.get(a, []):
+                step(other)
+            gradient(a)
+            for step, other in between.get(a, []):
+                step(other)
+            quantise_dproj(a)
+            multiply_and_store(a)

@@ -26,7 +26,7 @@ TYPES_PER_ATTR_LOAD = 4
 ATTR_LOADS = TYPES // TYPES_PER_ATTR_LOAD
 VECTOR_PLACES = (64, 48)
 LINE = 2
-STORES = ((0, 1, 2), (3, 4), (5,), (6,), (7,))
+STORES = ((0, 1, 2), (3,), (4,), (5,), (6,), (7,))
 DMA_ALIGN = 256
 
 FLOPS = 2 * TYPES * REP * PROJ * NODES
@@ -184,9 +184,9 @@ def tile_attributegnn_pb_v_kernel(
         for a in range(TYPES_PER_ATTR_LOAD):
             regroup_attr(a)
         grad_grouped = consts.tile([PART, PROJ, PACK], BF16)
-        nc.scalar.copy(
-            out=grad_grouped[:].rearrange("p (w i) t -> p w t i", i=LINE * PACK),
-            in_=grad_rows[:].rearrange("p t (w i) -> p w t i", i=LINE * PACK),
+        nc.vector.tensor_copy(
+            out=grad_grouped[:].rearrange("p (w i) t -> p w t i", i=RUN),
+            in_=grad_rows[:].rearrange("p t (w i) -> p w t i", i=RUN),
         )
         quantise_attr(0)
         quantise_attr(1)
@@ -200,7 +200,6 @@ def tile_attributegnn_pb_v_kernel(
         )
         nc.vector.tensor_copy(out=weight[:], in_=acc[:, :TYPES])
         quantise_attr(2)
-        quantise_attr(3)
         weighted_gate(0)
 
         before = {
@@ -212,6 +211,7 @@ def tile_attributegnn_pb_v_kernel(
             6: [(quantise_attr, 6)],
         }
         between = {
+            0: [(quantise_attr, 3)],
             1: [(weighted_gate, 2)],
             2: [(regroup_attr, 4)],
             3: [(regroup_attr, 6)],

from contextlib import ExitStack

import concourse.mybir as mybir
from concourse.masks import make_identity

BF16 = mybir.dt.bfloat16
F32 = mybir.dt.float32
U32 = mybir.dt.uint32
U8 = mybir.dt.uint8
E4M3_X4 = mybir.dt.float8_e4m3fn_x4
E5M2_X4 = mybir.dt.float8_e5m2_x4
ALU = mybir.AluOpType

NODES = 512
TYPES = 8
REP = 512
PROJ = 512

PART = 128
PACK = 4
RUN = 4
ROW_TILES = REP // PART
TYPES_PER_LOAD = 2
LOADS = TYPES // TYPES_PER_LOAD
TYPES_PER_ATTR_LOAD = 4
ATTR_LOADS = TYPES // TYPES_PER_ATTR_LOAD
VECTOR_PLACES = (64, 48)
LINE = 2
STORES = ((0, 1, 2), (3,), (4,), (5,), (6,), (7,))
DMA_ALIGN = 256

FLOPS = 2 * TYPES * REP * PROJ * NODES
BYTES = 2 * NODES * TYPES * REP + 2 * TYPES + 4 * NODES * TYPES * PROJ + 2 * NODES * PROJ + 4 * TYPES * REP * PROJ

assert NODES == PART * PACK
assert TYPES_PER_LOAD == 2


def tile_attributegnn_pb_v_kernel(
    tc, attr_rep, bwd_proj, self_weighted, proj, grad_out, out
):
    nc = tc.nc
    attr_by_partition = attr_rep.rearrange("(p t) a r -> p t a r", t=PACK)
    proj_by_partition = proj.rearrange("(p t) a c -> p t a c", t=PACK)

    with ExitStack() as ctx:
        consts = ctx.enter_context(tc.tile_pool(name="consts", bufs=1))
        loads = ctx.enter_context(tc.tile_pool(name="loads", bufs=LOADS))
        attr_pool = ctx.enter_context(tc.tile_pool(name="attr_pool", bufs=ATTR_LOADS))
        on_vector = ctx.enter_context(tc.tile_pool(name="on_vector", bufs=TYPES_PER_LOAD))
        shared = ctx.enter_context(tc.tile_pool(name="shared", bufs=2 * TYPES_PER_LOAD))
        results = ctx.enter_context(tc.tile_pool(name="results", bufs=1))
        psum = ctx.enter_context(tc.psum_pool(name="psum", bufs=8))
        ctx.enter_context(tc.manual_schedule())

        identity = consts.tile([PART, PART], BF16)
        weight_column = consts.tile([PART, 1], BF16)
        nc.gpsimd.memset(weight_column[:], 0.0)
        nc.scalar.dma_start(
            out=weight_column[0:TYPES, :], in_=self_weighted.rearrange("o a u -> (o a) u")
        )
        make_identity(nc, identity[:])
        grad_rows = consts.tile([PART, PACK, PROJ], BF16, align_bytes=DMA_ALIGN)
        attr_loads = []
        proj_loads = []

        def load_attr(load):
            types = slice(load * TYPES_PER_ATTR_LOAD, (load + 1) * TYPES_PER_ATTR_LOAD)
            attr_rows = attr_pool.tile(
                [PART, PACK, TYPES_PER_ATTR_LOAD, REP], BF16, align_bytes=DMA_ALIGN
            )
            nc.sync.dma_start(out=attr_rows[:], in_=attr_by_partition[:, :, types, :])
            attr_loads.append(attr_rows)

        def load_proj(load):
            types = slice(load * TYPES_PER_LOAD, (load + 1) * TYPES_PER_LOAD)
            proj_rows = loads.tile([PART, PACK, TYPES_PER_LOAD, PROJ], F32, align_bytes=DMA_ALIGN)
            nc.sync.dma_start(out=proj_rows[:], in_=proj_by_partition[:, :, types, :])
            proj_loads.append(proj_rows)

        load_attr(0)
        nc.sync.dma_start(out=grad_rows[:], in_=grad_out.rearrange("(p t) c -> p t c", t=PACK))
        load_proj(0)
        load_proj(1)
        load_attr(1)
        load_proj(2)
        load_proj(3)

        weight = consts.tile([PART, TYPES], F32)

        attr_grouped_of = {}
        gate_of = {}
        dproj_of = {}
        attr_mx_of = {}
        dproj_mx_of = {}
        result_of = {}

        def weighted_gate(a):
            gate = on_vector.tile([PART, PROJ, PACK], BF16)
            proj_rows = proj_loads[a // TYPES_PER_LOAD][:, :, a % TYPES_PER_LOAD, :]
            nc.vector.tensor_scalar(
                out=gate[:].rearrange("p (w i) t -> p w t i", i=RUN),
                in0=proj_rows.rearrange("p t (w i) -> p w t i", i=RUN),
                scalar1=0.0,
                scalar2=weight[:, a : a + 1],
                op0=ALU.is_gt,
                op1=ALU.mult,
            )
            gate_of[a] = gate

        def gradient(a):
            dproj = on_vector.tile([PART, PROJ * PACK], BF16, align_bytes=64)
            nc.vector.tensor_tensor(
                out=dproj[:],
                in0=gate_of[a][:].rearrange("p w t -> p (w t)"),
                in1=grad_grouped[:].rearrange("p w t -> p (w t)"),
                op=ALU.mult,
            )
            dproj_of[a] = dproj

        def regroup_attr(a):
            attr_grouped = shared.tile([PART, ROW_TILES, PART, PACK], BF16, align_bytes=64)
            attr_rows = attr_loads[a // TYPES_PER_ATTR_LOAD][:, :, a % TYPES_PER_ATTR_LOAD, :]
            by_line = attr_rows.rearrange("p t (w i m) -> p w t i m", i=LINE, m=ROW_TILES)
            grouped_by_line = attr_grouped[:].rearrange("p m (w i) t -> p w t i m", i=LINE)
            cut = VECTOR_PLACES[a // TYPES_PER_ATTR_LOAD] // LINE
            nc.vector.tensor_copy(out=grouped_by_line[:, :cut], in_=by_line[:, :cut])
            nc.scalar.copy(out=grouped_by_line[:, cut:], in_=by_line[:, cut:])
            attr_grouped_of[a] = attr_grouped

        def quantise_dproj(a):
            dproj_codes = shared.tile([PART, PROJ], U32, align_bytes=64)
            dproj_scales = shared.tile([PART, PROJ], U8, align_bytes=64)
            nc.vector.quantize_mx(
                out=dproj_codes[:].bitcast(E5M2_X4),
                scales=dproj_scales[:],
                in_=dproj_of[a][:],
            )
            dproj_mx_of[a] = (dproj_codes, dproj_scales)

        def quantise_attr(a):
            attr_codes = shared.tile([PART, REP], U32, align_bytes=64)
            attr_scales = shared.tile([PART, REP], U8, align_bytes=64)
            nc.vector.quantize_mx(
                out=attr_codes[:].bitcast(E4M3_X4),
                scales=attr_scales[:],
                in_=attr_grouped_of[a][:].rearrange("p m w t -> p (m w t)"),
            )
            attr_mx_of[a] = (attr_codes, attr_scales)

        def multiply_and_store(a):
            attr_codes, attr_scales = attr_mx_of[a]
            dproj_codes, dproj_scales = dproj_mx_of[a]
            group = [types for types in STORES if a in types][0]
            first, count = group[0], len(group)
            if a == first:
                result_of[first] = results.tile(
                    [PART, count, ROW_TILES, PROJ], F32, align_bytes=DMA_ALIGN, name="result_%d" % first
                )
            result = result_of[first][:, a - first]
            last = a == TYPES - 1
            for m in range(ROW_TILES):
                places = slice(m * PART, (m + 1) * PART)
                acc = psum.tile([PART, PROJ], F32)
                nc.tensor.matmul_mx(
                    out=acc[:],
                    lhsT=attr_codes[:, places].bitcast(E4M3_X4),
                    lhsT_scale=attr_scales[:, places],
                    rhs=dproj_codes[:].bitcast(E5M2_X4),
                    rhs_scale=dproj_scales[:],
                    start=True,
                    stop=True,
                )
                if last and m % 2 == 1:
                    nc.vector.tensor_copy(out=result[:, m, :], in_=acc[:])
                else:
                    nc.scalar.copy(out=result[:, m, :], in_=acc[:])
            if a == first + count - 1:
                nc.sync.dma_start(
                    out=out[first : first + count].rearrange("a (p m) c -> p a m c", m=ROW_TILES),
                    in_=result_of[first][:],
                )

        for a in range(TYPES_PER_ATTR_LOAD):
            regroup_attr(a)
        grad_grouped = consts.tile([PART, PROJ, PACK], BF16)
        nc.vector.tensor_copy(
            out=grad_grouped[:].rearrange("p (w i) t -> p w t i", i=RUN),
            in_=grad_rows[:].rearrange("p t (w i) -> p w t i", i=RUN),
        )
        quantise_attr(0)
        quantise_attr(1)
        acc = psum.tile([PART, PROJ], F32)
        nc.tensor.matmul(
            out=acc[:, :TYPES],
            lhsT=weight_column[:, 0:1].to_broadcast([PART, PART]),
            rhs=identity[:, :TYPES],
            start=True,
            stop=True,
        )
        nc.vector.tensor_copy(out=weight[:], in_=acc[:, :TYPES])
        quantise_attr(2)
        weighted_gate(0)

        before = {
            0: [(weighted_gate, 1)],
            2: [(weighted_gate, 3)],
            3: [(regroup_attr, 5)],
            4: [(weighted_gate, 4), (quantise_attr, 4)],
            5: [(regroup_attr, 7), (quantise_attr, 5)],
            6: [(quantise_attr, 6)],
        }
        between = {
            0: [(quantise_attr, 3)],
            1: [(weighted_gate, 2)],
            2: [(regroup_attr, 4)],
            3: [(regroup_attr, 6)],
            4: [(weighted_gate, 5)],
            5: [(weighted_gate, 6)],
            6: [(weighted_gate, 7)],
            7: [(quantise_attr, 7)],
        }
        for a in range(TYPES):
            for step, other in before.get(a, []):
                step(other)
            gradient(a)
            for step, other in between.get(a, []):
                step(other)
            quantise_dproj(a)
            multiply_and_store(a)
